import numpy as np
import ml_dtypes


def mxq(x, axis, fmt="e4m3"):
    dtype, down = {"e4m3": (ml_dtypes.float8_e4m3fn, 7), "e5m2": (ml_dtypes.float8_e5m2, 14)}[fmt]
    v = np.moveaxis(np.asarray(x, np.float32).astype(ml_dtypes.bfloat16).astype(np.float64), axis, -1)
    blocks = v.reshape(v.shape[:-1] + (-1, 32))
    amax = np.abs(blocks).max(-1, keepdims=True)
    byte = np.maximum(np.where(amax > 0, np.frexp(amax)[1] - 1 + 127, 0) - down, 1)
    scale = np.exp2(byte - 127.0)
    codes = (blocks / scale).astype(np.float32).astype(dtype).astype(np.float64)
    return np.moveaxis((codes * scale).reshape(v.shape), -1, axis)


WIDE = False


def mx_kscale(k):
    if not WIDE:
        return np.ones(k)
    levels = np.array([10, -10, 5, -5, 0])
    a = np.random.permutation(np.resize(levels, k // 512 * 4)).reshape(k // 512, 4)
    idx = np.arange(k)
    return np.exp2(a[idx // 512, idx % 128 // 32])


BF16 = ml_dtypes.bfloat16


def bf(x):
    return np.asarray(x, np.float32).astype(BF16)


def f64(x):
    return np.asarray(x).astype(np.float64)


B, N, DIN, DH, DOUT = 4096, 8, 64, 64, 64
KH = N * DH
KO = N * DOUT
EPS = 1e-5


def elu(v):
    return np.where(v > 0.0, v, np.expm1(np.minimum(v, 0.0)))


def sigmoid(v):
    return 1.0 / (1.0 + np.exp(-v))


def setup_inputs():
    rn = np.random.standard_normal
    s, t = mx_kscale(KH), mx_kscale(KO)
    return {
        "h": bf(elu(rn((B, KH))) * s),
        "x": bf(rn((B, N, DIN)) + 0.5),
        "cW1": bf(rn((KH, KO)) * 1.2 / np.sqrt(KH) / s[:, None] * t),
        "cb1": bf(rn(KO) * 0.3 * t),
        "cW4": bf(rn((KO, KO)) / np.sqrt(KO) / t[:, None]),
        "cb4": bf(rn(KO) * 0.3),
        "cW5": bf(rn((KO, KO)) / np.sqrt(KO) / t[:, None]),
        "cb5": bf(rn(KO) * 0.3),
        "clng": bf(1.0 + 0.2 * rn(KO)),
        "clnb": bf(0.2 * rn(KO)),
    }


def reference(h, x, cW1, cb1, cW4, cb4, cW5, cb5, clng, clnb):
    flat = f64(x).reshape(B, N * DIN)
    e1 = (mxq(f64(h), 1, "e4m3") @ mxq(f64(cW1), 0, "e4m3")) + f64(cb1)
    e1q = mxq(e1, 1, "e4m3")
    g = sigmoid((e1q @ mxq(f64(cW4), 0, "e4m3")) + f64(cb4)) * ((e1q @ mxq(f64(cW5), 0, "e4m3")) + f64(cb5))
    r = flat + g
    c = (r - r.mean(-1, keepdims=True)) * (1.0 / np.sqrt(r.var(-1, keepdims=True) + EPS)) * f64(clng) + f64(clnb)
    c = c.reshape(B, N, DOUT)
    e = np.exp(c - c.max(1, keepdims=True))
    return e / e.sum(1, keepdims=True)

@@ -1,0 +1,333 @@
+from contextlib import ExitStack
+
+import concourse.mybir as mybir
+from concourse.masks import make_identity
+
+F32 = mybir.dt.float32
+BF16 = mybir.dt.bfloat16
+U32 = mybir.dt.uint32
+U8 = mybir.dt.uint8
+FP8X4 = mybir.dt.float8_e4m3fn_x4
+ALU = mybir.AluOpType
+ACT = mybir.ActivationFunctionType
+
+P = 128
+PACK = 4
+B = 4096
+WIDTH = 512
+N_VAR = 8
+D_FEAT = 64
+CHUNK = 512
+ROW_TILES = CHUNK // P
+FEAT_TILES = WIDTH // P
+N_CHUNKS = B // CHUNK
+EPS = 1e-5
+
+FLOPS = 3 * 2 * B * WIDTH * WIDTH
+
+
+def tile_variableselectionnetwork_pa_t_kernel(
+    tc, h, x, cW1, cb1, cW4, cb4, cW5, cb5, clng, clnb, out
+):
+    nc = tc.nc
+    with ExitStack() as ctx:
+        consts = ctx.enter_context(tc.tile_pool(name="consts", bufs=1))
+        setup = ctx.enter_context(tc.tile_pool(name="setup", bufs=1))
+        io = ctx.enter_context(tc.tile_pool(name="io", bufs=3))
+        work = ctx.enter_context(tc.tile_pool(name="work", bufs=2))
+        gate = ctx.enter_context(tc.tile_pool(name="gate", bufs=2))
+        tail = ctx.enter_context(tc.tile_pool(name="tail", bufs=2))
+        psum = ctx.enter_context(tc.psum_pool(name="psum", bufs=2))
+
+        def load_chunk(c):
+            rows = slice(c * CHUNK, (c + 1) * CHUNK)
+            h_sb = io.tile([P, ROW_TILES, WIDTH], BF16, name="h_sb", tag="h_sb")
+            nc.sync.dma_start(out=h_sb[:], in_=h[rows, :].rearrange("(p a) k -> p a k", a=ROW_TILES))
+            x_sb = io.tile([P, ROW_TILES, WIDTH], BF16, name="x_sb", tag="x_sb")
+            nc.sync.dma_start(
+                out=x_sb[:], in_=x[rows, :, :].rearrange("(p a) n d -> p a (n d)", a=ROW_TILES)
+            )
+            return h_sb, x_sb
+
+        w1_raw = setup.tile([P, PACK, WIDTH], BF16, name="w1_raw")
+        nc.sync.dma_start(
+            out=w1_raw[:].rearrange("q (u e) c -> q u (e c)", u=2),
+            in_=cW1.rearrange("(u q e) c -> q u (e c)", u=2, e=2),
+        )
+        loaded = {0: load_chunk(0)}
+        bias_rows = setup.tile([P, P], BF16, name="bias_rows")
+        nc.vector.memset(bias_rows[:], 0.0)
+        for i, vec in enumerate((cb1, cb4, cb5)):
+            nc.sync.dma_start(
+                out=bias_rows[FEAT_TILES * i : FEAT_TILES * (i + 1), :],
+                in_=vec.rearrange("(t p) -> t p", p=P),
+            )
+        w4_raw = setup.tile([P, PACK, WIDTH], BF16, name="w4_raw")
+        nc.sync.dma_start(out=w4_raw[:], in_=cW4.rearrange("(t p) c -> p t c", p=P))
+        w5_raw = setup.tile([P, PACK, WIDTH], BF16, name="w5_raw")
+        nc.sync.dma_start(out=w5_raw[:], in_=cW5.rearrange("(t p) c -> p t c", p=P))
+        clng_bc = consts.tile([P, WIDTH], BF16, name="clng_bc")
+        nc.gpsimd.dma_start(out=clng_bc[:], in_=clng.partition_broadcast(P))
+        clnb_bc = consts.tile([P, WIDTH], BF16, name="clnb_bc")
+        nc.gpsimd.dma_start(out=clnb_bc[:], in_=clnb.partition_broadcast(P))
+
+        ident_f32 = consts.tile([P, P], F32, name="ident_f32")
+        make_identity(nc, ident_f32[:])
+        ident_bf16 = consts.tile([P, P], BF16, name="ident_bf16")
+        make_identity(nc, ident_bf16[:])
+        swap_f32 = consts.tile([P, P], F32, name="swap_f32")
+        nc.vector.tensor_copy(out=swap_f32[:, 0:D_FEAT], in_=ident_f32[:, D_FEAT:P])
+        nc.vector.tensor_copy(out=swap_f32[:, D_FEAT:P], in_=ident_f32[:, 0:D_FEAT])
+        neg_half = consts.tile([P, ROW_TILES], F32, name="neg_half")
+        nc.vector.memset(neg_half[:], -0.5)
+
+        def quantise_weight(raw, copy, name):
+            grouped = setup.tile([P, WIDTH, PACK], BF16, name=name + "_grouped", align_bytes=64)
+            copy(
+                out=grouped[:].rearrange("p (c i) t -> p c t i", i=4),
+                in_=raw[:].rearrange("p t (c i) -> p c t i", i=4),
+            )
+            codes = consts.tile([P, WIDTH], U32, name=name + "_codes", align_bytes=64)
+            scales = consts.tile([P, WIDTH], U8, name=name + "_scales", align_bytes=64)
+            nc.vector.quantize_mx(
+                out=codes[:].bitcast(FP8X4),
+                scales=scales[:],
+                in_=grouped[:].rearrange("p c t -> p (c t)"),
+            )
+            return codes, scales
+
+        w1_codes, w1_scales = quantise_weight(w1_raw, nc.vector.tensor_copy, "w1")
+        w4_codes, w4_scales = quantise_weight(w4_raw, nc.scalar.copy, "w4")
+        w5_codes, w5_scales = quantise_weight(w5_raw, nc.scalar.copy, "w5")
+
+        bias_ps = psum.tile([P, P], BF16, name="bias_ps", tag="hT_ps", bufs=1)
+        nc.tensor.transpose(bias_ps[:], bias_rows[:], ident_bf16[:])
+        bias_cols = consts.tile([P, 3 * FEAT_TILES], F32, name="bias_cols")
+        nc.vector.tensor_copy(out=bias_cols[:], in_=bias_ps[:, 0 : 3 * FEAT_TILES])
+        cb1_cols = bias_cols[:, 0:FEAT_TILES]
+        half_cb45_cols = consts.tile([P, 2 * FEAT_TILES], F32, name="half_cb45_cols")
+        nc.vector.tensor_scalar_mul(
+            out=half_cb45_cols[:], in0=bias_cols[:, FEAT_TILES : 3 * FEAT_TILES], scalar1=0.5
+        )
+        half_cb4_cols = half_cb45_cols[:, 0:FEAT_TILES]
+        half_cb5_cols = half_cb45_cols[:, FEAT_TILES : 2 * FEAT_TILES]
+
+        def max_over_variables(src):
+            width = WIDTH
+            while width > D_FEAT:
+                width //= 2
+                dst = tail.tile([P, ROW_TILES, width], BF16, name="c_max_%d" % width)
+                nc.vector.tensor_tensor(
+                    out=dst[:], in0=src[:, :, 0:width], in1=src[:, :, width : 2 * width], op=ALU.max
+                )
+                src = dst
+            return src
+
+        def over_variables(per_feature):
+            return per_feature.unsqueeze(2).to_broadcast([P, ROW_TILES, N_VAR, D_FEAT])
+
+        def by_variable(tile_ap):
+            return tile_ap.rearrange("p a (n d) -> p a n d", n=N_VAR)
+
+        def chunk_to_exponentials(c):
+            if c + 1 < N_CHUNKS:
+                loaded[c + 1] = load_chunk(c + 1)
+            h_sb, x_sb = loaded[c]
+
+            h_grouped = work.tile([P, CHUNK * PACK], BF16, name="h_grouped", align_bytes=64)
+            h_grouped_words = h_grouped[:].bitcast(F32).rearrange(
+                "q (a b u) -> q a b u", a=ROW_TILES, u=2
+            )
+            for pair in range(ROW_TILES // 2):
+                hT_ps = psum.tile([P, 2, 2, P], F32, name="hT_ps", tag="hT_ps", bufs=1)
+                for a in range(2):
+                    h_words = h_sb[:, 2 * pair + a, :].bitcast(F32)
+                    for u in range(2):
+                        nc.tensor.transpose(
+                            hT_ps[:, a, u, :], h_words[:, u * P : (u + 1) * P], ident_f32[:]
+                        )
+                nc.scalar.copy(
+                    out=h_grouped_words[:, 2 * pair : 2 * pair + 2, :, :],
+                    in_=hT_ps[:].rearrange("q a u b -> q a b u"),
+                )
+            h_codes = work.tile([P, CHUNK], U32, name="h_codes", align_bytes=64)
+            h_scales = work.tile([P, CHUNK], U8, name="h_scales", align_bytes=64)
+            nc.vector.quantize_mx(out=h_codes[:].bitcast(FP8X4), scales=h_scales[:], in_=h_grouped[:])
+
+            e1_grouped = work.tile([P, CHUNK, PACK], BF16, name="e1_grouped", align_bytes=64)
+            for a in range(ROW_TILES):
+                cols = slice(a * P, (a + 1) * P)
+                e1_ps = psum.tile([P, PACK, P], F32, name="e1_ps", tag="e1_ps")
+                for t in range(PACK):
+                    feats = slice(t * P, (t + 1) * P)
+                    nc.tensor.matmul_mx(
+                        out=e1_ps[:, t, :],
+                        lhsT=w1_codes[:, feats].bitcast(FP8X4),
+                        lhsT_scale=w1_scales[:, feats],
+                        rhs=h_codes[:, cols].bitcast(FP8X4),
+                        rhs_scale=h_scales[:, cols],
+                        start=True,
+                        stop=True,
+                    )
+                nc.vector.tensor_tensor(
+                    out=e1_grouped[:, cols, :],
+                    in0=e1_ps[:].rearrange("p t b -> p b t"),
+                    in1=cb1_cols.unsqueeze(1).to_broadcast([P, P, PACK]),
+                    op=ALU.add,
+                )
+            e1_codes = work.tile([P, CHUNK], U32, name="e1_codes", align_bytes=64)
+            e1_scales = work.tile([P, CHUNK], U8, name="e1_scales", align_bytes=64)
+            nc.vector.quantize_mx(
+                out=e1_codes[:].bitcast(FP8X4),
+                scales=e1_scales[:],
+                in_=e1_grouped[:].rearrange("p b t -> p (b t)"),
+            )
+
+            gT = gate.tile([P, FEAT_TILES, CHUNK], F32, name="gT")
+            for j2 in range(0, FEAT_TILES, 2):
+                tanh_sb = gate.tile([P, 2, CHUNK], F32, name="tanh_sb")
+                half_lin_sb = gate.tile([P, 2, CHUNK], F32, name="half_lin_sb")
+                for i in range(2):
+                    j = j2 + i
+                    feats = slice(j * P, (j + 1) * P)
+                    u4_ps = psum.tile([P, CHUNK], F32, name="u4_ps", tag="u_ps")
+                    u5_ps = psum.tile([P, CHUNK], F32, name="u5_ps", tag="u_ps")
+                    for u_ps, codes, scales in ((u4_ps, w4_codes, w4_scales), (u5_ps, w5_codes, w5_scales)):
+                        nc.tensor.matmul_mx(
+                            out=u_ps[:],
+                            lhsT=codes[:, feats].bitcast(FP8X4),
+                            lhsT_scale=scales[:, feats],
+                            rhs=e1_codes[:].bitcast(FP8X4),
+                            rhs_scale=e1_scales[:],
+                            start=True,
+                            stop=True,
+                        )
+                    nc.scalar.activation(
+                        out=tanh_sb[:, i, :], in_=u4_ps[:], func=ACT.Tanh, bias=half_cb4_cols[:, j : j + 1], scale=0.5
+                    )
+                    nc.scalar.activation(
+                        out=half_lin_sb[:, i, :],
+                        in_=u5_ps[:],
+                        func=ACT.Identity,
+                        bias=half_cb5_cols[:, j : j + 1],
+                        scale=0.5,
+                    )
+                nc.vector.scalar_tensor_tensor(
+                    out=gT[:, j2 : j2 + 2, :], in0=tanh_sb[:], scalar=1.0, in1=half_lin_sb[:], op0=ALU.add, op1=ALU.mult
+                )
+
+            r_sb = tail.tile([P, ROW_TILES, WIDTH], F32, name="r_sb")
+            r_sum = tail.tile([P, ROW_TILES], F32, name="r_sum")
+            for a in range(ROW_TILES):
+                r_ps = psum.tile([P, WIDTH], F32, name="r_ps", tag="r_ps")
+                for j in range(FEAT_TILES):
+                    feats = slice(j * P, (j + 1) * P)
+                    nc.tensor.matmul(
+                        out=r_ps[:, feats], lhsT=ident_bf16[:], rhs=x_sb[:, a, feats], start=True, stop=False
+                    )
+                    nc.tensor.matmul(
+                        out=r_ps[:, feats],
+                        lhsT=gT[:, j, a * P : (a + 1) * P],
+                        rhs=ident_f32[:],
+                        start=False,
+                        stop=True,
+                        is_transpose=True,
+                    )
+                nc.scalar.activation(
+                    out=r_sb[:, a, :], in_=r_ps[:], func=ACT.Identity, accum_out=r_sum[:, a : a + 1]
+                )
+
+            neg_mean = tail.tile([P, ROW_TILES], F32, name="neg_mean")
+            nc.gpsimd.tensor_scalar(
+                out=neg_mean[:], in0=r_sum[:], scalar1=-1.0 / WIDTH, scalar2=0.0, op0=ALU.mult, op1=ALU.add
+            )
+            squares = tail.tile([P, ROW_TILES, WIDTH], BF16, name="squares")
+            dev_sq_sum = tail.tile([P, ROW_TILES], F32, name="dev_sq_sum")
+            for a in range(ROW_TILES):
+                nc.scalar.activation(
+                    out=squares[:, a, :],
+                    in_=r_sb[:, a, :],
+                    func=ACT.Square,
+                    bias=neg_mean[:, a : a + 1],
+                    scale=1.0,
+                    accum_out=dev_sq_sum[:, a : a + 1],
+                )
+            var_eps = tail.tile([P, ROW_TILES], F32, name="var_eps")
+            nc.gpsimd.tensor_scalar(
+                out=var_eps[:], in0=dev_sq_sum[:], scalar1=1.0 / WIDTH, scalar2=EPS, op0=ALU.mult, op1=ALU.add
+            )
+            rstd = tail.tile([P, ROW_TILES], F32, name="rstd")
+            nc.gpsimd.tensor_tensor(out=rstd[:], in0=var_eps[:], in1=neg_half[:], op=ALU.pow)
+
+            c_sb = tail.tile([P, ROW_TILES, WIDTH], F32, name="c_sb", bufs=4)
+            for a in range(ROW_TILES):
+                nc.vector.scalar_tensor_tensor(
+                    out=c_sb[:, a, :],
+                    in0=r_sb[:, a, :],
+                    scalar=neg_mean[:, a : a + 1],
+                    in1=clng_bc[:],
+                    op0=ALU.add,
+                    op1=ALU.mult,
+                )
+            for a in range(ROW_TILES):
+                nc.vector.scalar_tensor_tensor(
+                    out=c_sb[:, a, :],
+                    in0=c_sb[:, a, :],
+                    scalar=rstd[:, a : a + 1],
+                    in1=clnb_bc[:],
+                    op0=ALU.mult,
+                    op1=ALU.add,
+                )
+
+            c_max = max_over_variables(c_sb)
+            nc.vector.tensor_tensor(
+                out=by_variable(c_sb[:]), in0=by_variable(c_sb[:]), in1=over_variables(c_max[:]), op=ALU.subtract
+            )
+            nc.scalar.activation(out=c_sb[:], in_=c_sb[:], func=ACT.Exp)
+
+            e_sumT_ps = psum.tile([P, ROW_TILES, P], F32, name="e_sumT_ps", tag="e_sum_ps", bufs=1)
+            for a in range(ROW_TILES):
+                for j in range(FEAT_TILES):
+                    nc.tensor.matmul(
+                        out=e_sumT_ps[:, a, :],
+                        lhsT=c_sb[:, a, j * P : (j + 1) * P],
+                        rhs=ident_f32[:],
+                        start=(j == 0),
+                        stop=(j == FEAT_TILES - 1),
+                        is_transpose=True,
+                    )
+            e_sumT = tail.tile([P, ROW_TILES, P], F32, name="e_sumT", bufs=4)
+            nc.scalar.copy(out=e_sumT[:], in_=e_sumT_ps[:])
+            return c_sb, e_sumT
+
+        for first in range(0, N_CHUNKS, 2):
+            exponentials = [chunk_to_exponentials(first + i) for i in range(2)]
+            e_sum_inv = tail.tile([P, 2, ROW_TILES, D_FEAT], F32, name="e_sum_inv")
+            for i in range(2):
+                e_sumT = exponentials[i][1]
+                e_sum_ps = psum.tile([P, ROW_TILES, P], F32, name="e_sum_ps", tag="e_sum_ps", bufs=1)
+                for a in range(ROW_TILES):
+                    for moving, first_of_group in ((ident_f32, True), (swap_f32, False)):
+                        nc.tensor.matmul(
+                            out=e_sum_ps[:, a, :],
+                            lhsT=e_sumT[:, a, :],
+                            rhs=moving[:],
+                            start=first_of_group,
+                            stop=not first_of_group,
+                            is_transpose=True,
+                        )
+                nc.scalar.activation(out=e_sum_inv[:, i, :, :], in_=e_sum_ps[:, :, 0:D_FEAT], func=ACT.Ln)
+            nc.scalar.activation(out=e_sum_inv[:], in_=e_sum_inv[:], func=ACT.Exp, scale=-1.0)
+            for i in range(2):
+                c = first + i
+                out_sb = tail.tile([P, ROW_TILES, WIDTH], F32, name="out_sb")
+                nc.vector.tensor_tensor(
+                    out=by_variable(out_sb[:]),
+                    in0=by_variable(exponentials[i][0][:]),
+                    in1=over_variables(e_sum_inv[:, i, :, :]),
+                    op=ALU.mult,
+                )
+                nc.sync.dma_start(
+                    out=out[c * CHUNK : (c + 1) * CHUNK, :, :].rearrange("(p a) n d -> p a (n d)", a=ROW_TILES),
+                    in_=out_sb[:],
+                )

@@ -75,9 +75,6 @@ def tile_variableselectionnetwork_pa_t_kernel(
         make_identity(nc, ident_f32[:])
         ident_bf16 = consts.tile([P, P], BF16, name="ident_bf16")
         make_identity(nc, ident_bf16[:])
-        swap_f32 = consts.tile([P, P], F32, name="swap_f32")
-        nc.vector.tensor_copy(out=swap_f32[:, 0:D_FEAT], in_=ident_f32[:, D_FEAT:P])
-        nc.vector.tensor_copy(out=swap_f32[:, D_FEAT:P], in_=ident_f32[:, 0:D_FEAT])
         neg_half = consts.tile([P, ROW_TILES], F32, name="neg_half")
         nc.vector.memset(neg_half[:], -0.5)
 
@@ -112,16 +109,16 @@ def tile_variableselectionnetwork_pa_t_kernel(
         half_cb4_cols = half_cb45_cols[:, 0:FEAT_TILES]
         half_cb5_cols = half_cb45_cols[:, FEAT_TILES : 2 * FEAT_TILES]
 
-        def max_over_variables(src):
-            width = WIDTH
+        def over_the_variables(src, op, dtype, name, last):
+            width = WIDTH // 2
             while width > D_FEAT:
-                width //= 2
-                dst = tail.tile([P, ROW_TILES, width], BF16, name="c_max_%d" % width)
+                dst = tail.tile([P, ROW_TILES, width], dtype, name="%s_%d" % (name, width))
                 nc.vector.tensor_tensor(
-                    out=dst[:], in0=src[:, :, 0:width], in1=src[:, :, width : 2 * width], op=ALU.max
+                    out=dst[:], in0=src[:, :, 0:width], in1=src[:, :, width : 2 * width], op=op
                 )
                 src = dst
-            return src
+                width //= 2
+            nc.vector.tensor_tensor(out=last, in0=src[:, :, 0:width], in1=src[:, :, width : 2 * width], op=op)
 
         def over_variables(per_feature):
             return per_feature.unsqueeze(2).to_broadcast([P, ROW_TILES, N_VAR, D_FEAT])
@@ -129,7 +126,7 @@ def tile_variableselectionnetwork_pa_t_kernel(
         def by_variable(tile_ap):
             return tile_ap.rearrange("p a (n d) -> p a n d", n=N_VAR)
 
-        def chunk_to_exponentials(c):
+        def chunk_to_exponentials(c, e_sum):
             if c + 1 < N_CHUNKS:
                 loaded[c + 1] = load_chunk(c + 1)
             h_sb, x_sb = loaded[c]
@@ -219,7 +216,7 @@ def tile_variableselectionnetwork_pa_t_kernel(
             r_sb = tail.tile([P, ROW_TILES, WIDTH], F32, name="r_sb")
             r_sum = tail.tile([P, ROW_TILES], F32, name="r_sum")
             for a in range(ROW_TILES):
-                r_ps = psum.tile([P, WIDTH], F32, name="r_ps", tag="r_ps")
+                r_ps = psum.tile([P, WIDTH], F32, name="r_ps", tag="r_ps", bufs=3)
                 for j in range(FEAT_TILES):
                     feats = slice(j * P, (j + 1) * P)
                     nc.tensor.matmul(
@@ -279,51 +276,26 @@ def tile_variableselectionnetwork_pa_t_kernel(
                     op1=ALU.add,
                 )
 
-            c_max = max_over_variables(c_sb)
+            c_max = tail.tile([P, ROW_TILES, D_FEAT], BF16, name="c_max")
+            over_the_variables(c_sb, ALU.max, BF16, "c_max", c_max[:])
             nc.vector.tensor_tensor(
                 out=by_variable(c_sb[:]), in0=by_variable(c_sb[:]), in1=over_variables(c_max[:]), op=ALU.subtract
             )
             nc.scalar.activation(out=c_sb[:], in_=c_sb[:], func=ACT.Exp)
-
-            e_sumT_ps = psum.tile([P, ROW_TILES, P], F32, name="e_sumT_ps", tag="e_sum_ps", bufs=1)
-            for a in range(ROW_TILES):
-                for j in range(FEAT_TILES):
-                    nc.tensor.matmul(
-                        out=e_sumT_ps[:, a, :],
-                        lhsT=c_sb[:, a, j * P : (j + 1) * P],
-                        rhs=ident_f32[:],
-                        start=(j == 0),
-                        stop=(j == FEAT_TILES - 1),
-                        is_transpose=True,
-                    )
-            e_sumT = tail.tile([P, ROW_TILES, P], F32, name="e_sumT", bufs=4)
-            nc.scalar.copy(out=e_sumT[:], in_=e_sumT_ps[:])
-            return c_sb, e_sumT
+            over_the_variables(c_sb, ALU.add, F32, "e_sum", e_sum)
+            return c_sb
 
         for first in range(0, N_CHUNKS, 2):
-            exponentials = [chunk_to_exponentials(first + i) for i in range(2)]
             e_sum_inv = tail.tile([P, 2, ROW_TILES, D_FEAT], F32, name="e_sum_inv")
-            for i in range(2):
-                e_sumT = exponentials[i][1]
-                e_sum_ps = psum.tile([P, ROW_TILES, P], F32, name="e_sum_ps", tag="e_sum_ps", bufs=1)
-                for a in range(ROW_TILES):
-                    for moving, first_of_group in ((ident_f32, True), (swap_f32, False)):
-                        nc.tensor.matmul(
-                            out=e_sum_ps[:, a, :],
-                            lhsT=e_sumT[:, a, :],
-                            rhs=moving[:],
-                            start=first_of_group,
-                            stop=not first_of_group,
-                            is_transpose=True,
-                        )
-                nc.scalar.activation(out=e_sum_inv[:, i, :, :], in_=e_sum_ps[:, :, 0:D_FEAT], func=ACT.Ln)
+            exponentials = [chunk_to_exponentials(first + i, e_sum_inv[:, i, :, :]) for i in range(2)]
+            nc.scalar.activation(out=e_sum_inv[:], in_=e_sum_inv[:], func=ACT.Ln)
             nc.scalar.activation(out=e_sum_inv[:], in_=e_sum_inv[:], func=ACT.Exp, scale=-1.0)
             for i in range(2):
                 c = first + i
                 out_sb = tail.tile([P, ROW_TILES, WIDTH], F32, name="out_sb")
                 nc.vector.tensor_tensor(
                     out=by_variable(out_sb[:]),
-                    in0=by_variable(exponentials[i][0][:]),
+                    in0=by_variable(exponentials[i][:]),
                     in1=over_variables(e_sum_inv[:, i, :, :]),
                     op=ALU.mult,
                 )

@@ -17,19 +17,27 @@ B = 4096
 WIDTH = 512
 N_VAR = 8
 D_FEAT = 64
-CHUNK = 512
-ROW_TILES = CHUNK // P
 FEAT_TILES = WIDTH // P
-N_CHUNKS = B // CHUNK
+MAX_ROW_TILES = 4
 EPS = 1e-5
 
 FLOPS = 3 * 2 * B * WIDTH * WIDTH
+
+
+def chunk_row_tiles():
+    ramp = [1]
+    while sum(ramp) < MAX_ROW_TILES:
+        ramp.append(sum(ramp))
+    n_full = (B // P - sum(ramp)) // MAX_ROW_TILES
+    return [MAX_ROW_TILES] * n_full + list(reversed(ramp))
 
 
 def tile_variableselectionnetwork_pa_t_kernel(
     tc, h, x, cW1, cb1, cW4, cb4, cW5, cb5, clng, clnb, out
 ):
     nc = tc.nc
+    sizes = chunk_row_tiles()
+    first_rows = [P * sum(sizes[:c]) for c in range(len(sizes))]
     with ExitStack() as ctx:
         consts = ctx.enter_context(tc.tile_pool(name="consts", bufs=1))
         setup = ctx.enter_context(tc.tile_pool(name="setup", bufs=1))
@@ -39,22 +47,25 @@ def tile_variableselectionnetwork_pa_t_kernel(
         tail = ctx.enter_context(tc.tile_pool(name="tail", bufs=2))
         psum = ctx.enter_context(tc.psum_pool(name="psum", bufs=2))
 
+        def rows_of(dram, c):
+            rows = slice(first_rows[c], first_rows[c] + P * sizes[c])
+            if dram.ndim == 3:
+                return dram[rows, :, :].rearrange("(p a) n d -> p a (n d)", a=sizes[c])
+            return dram[rows, :].rearrange("(p a) k -> p a k", a=sizes[c])
+
         def load_chunk(c):
-            rows = slice(c * CHUNK, (c + 1) * CHUNK)
-            h_sb = io.tile([P, ROW_TILES, WIDTH], BF16, name="h_sb", tag="h_sb")
-            nc.sync.dma_start(out=h_sb[:], in_=h[rows, :].rearrange("(p a) k -> p a k", a=ROW_TILES))
-            x_sb = io.tile([P, ROW_TILES, WIDTH], BF16, name="x_sb", tag="x_sb")
-            nc.sync.dma_start(
-                out=x_sb[:], in_=x[rows, :, :].rearrange("(p a) n d -> p a (n d)", a=ROW_TILES)
-            )
+            h_sb = io.tile([P, sizes[c], WIDTH], BF16, name="h_sb", tag="h_sb")
+            nc.sync.dma_start(out=h_sb[:], in_=rows_of(h, c))
+            x_sb = io.tile([P, sizes[c], WIDTH], BF16, name="x_sb", tag="x_sb")
+            nc.sync.dma_start(out=x_sb[:], in_=rows_of(x, c))
             return h_sb, x_sb
 
+        loaded = {0: load_chunk(0)}
         w1_raw = setup.tile([P, PACK, WIDTH], BF16, name="w1_raw")
         nc.sync.dma_start(
             out=w1_raw[:].rearrange("q (u e) c -> q u (e c)", u=2),
             in_=cW1.rearrange("(u q e) c -> q u (e c)", u=2, e=2),
         )
-        loaded = {0: load_chunk(0)}
         bias_rows = setup.tile([P, P], BF16, name="bias_rows")
         nc.vector.memset(bias_rows[:], 0.0)
         for i, vec in enumerate((cb1, cb4, cb5)):
@@ -75,7 +86,10 @@ def tile_variableselectionnetwork_pa_t_kernel(
         make_identity(nc, ident_f32[:])
         ident_bf16 = consts.tile([P, P], BF16, name="ident_bf16")
         make_identity(nc, ident_bf16[:])
-        neg_half = consts.tile([P, ROW_TILES], F32, name="neg_half")
+        swap_f32 = consts.tile([P, P], F32, name="swap_f32")
+        nc.vector.tensor_copy(out=swap_f32[:, 0:D_FEAT], in_=ident_f32[:, D_FEAT:P])
+        nc.vector.tensor_copy(out=swap_f32[:, D_FEAT:P], in_=ident_f32[:, 0:D_FEAT])
+        neg_half = consts.tile([P, MAX_ROW_TILES], F32, name="neg_half")
         nc.vector.memset(neg_half[:], -0.5)
 
         def quantise_weight(raw, copy, name):
@@ -109,50 +123,51 @@ def tile_variableselectionnetwork_pa_t_kernel(
         half_cb4_cols = half_cb45_cols[:, 0:FEAT_TILES]
         half_cb5_cols = half_cb45_cols[:, FEAT_TILES : 2 * FEAT_TILES]
 
-        def over_the_variables(src, op, dtype, name, last):
-            width = WIDTH // 2
+        def max_over_variables(src, row_tiles):
+            width = WIDTH
             while width > D_FEAT:
-                dst = tail.tile([P, ROW_TILES, width], dtype, name="%s_%d" % (name, width))
+                width //= 2
+                dst = tail.tile([P, row_tiles, width], BF16, name="c_max_%d" % width)
                 nc.vector.tensor_tensor(
-                    out=dst[:], in0=src[:, :, 0:width], in1=src[:, :, width : 2 * width], op=op
+                    out=dst[:], in0=src[:, :, 0:width], in1=src[:, :, width : 2 * width], op=ALU.max
                 )
                 src = dst
-                width //= 2
-            nc.vector.tensor_tensor(out=last, in0=src[:, :, 0:width], in1=src[:, :, width : 2 * width], op=op)
+            return src
 
         def over_variables(per_feature):
-            return per_feature.unsqueeze(2).to_broadcast([P, ROW_TILES, N_VAR, D_FEAT])
+            return per_feature.unsqueeze(2).to_broadcast([P, per_feature.shape[1], N_VAR, D_FEAT])
 
         def by_variable(tile_ap):
             return tile_ap.rearrange("p a (n d) -> p a n d", n=N_VAR)
 
-        def chunk_to_exponentials(c, e_sum):
-            if c + 1 < N_CHUNKS:
+        def chunk_to_exponentials(c):
+            row_tiles = sizes[c]
+            n_rows = P * row_tiles
+            if c + 1 < len(sizes):
                 loaded[c + 1] = load_chunk(c + 1)
             h_sb, x_sb = loaded[c]
 
-            h_grouped = work.tile([P, CHUNK * PACK], BF16, name="h_grouped", align_bytes=64)
-            h_grouped_words = h_grouped[:].bitcast(F32).rearrange(
-                "q (a b u) -> q a b u", a=ROW_TILES, u=2
-            )
-            for pair in range(ROW_TILES // 2):
-                hT_ps = psum.tile([P, 2, 2, P], F32, name="hT_ps", tag="hT_ps", bufs=1)
-                for a in range(2):
-                    h_words = h_sb[:, 2 * pair + a, :].bitcast(F32)
+            h_grouped = work.tile([P, n_rows * PACK], BF16, name="h_grouped", align_bytes=64)
+            h_grouped_words = h_grouped[:].bitcast(F32).rearrange("q (a b u) -> q a b u", a=row_tiles, u=2)
+            for a0 in range(0, row_tiles, 2):
+                n_tiles = min(2, row_tiles - a0)
+                hT_ps = psum.tile([P, n_tiles, 2, P], F32, name="hT_ps", tag="hT_ps", bufs=1)
+                for a in range(n_tiles):
+                    h_words = h_sb[:, a0 + a, :].bitcast(F32)
                     for u in range(2):
                         nc.tensor.transpose(
                             hT_ps[:, a, u, :], h_words[:, u * P : (u + 1) * P], ident_f32[:]
                         )
                 nc.scalar.copy(
-                    out=h_grouped_words[:, 2 * pair : 2 * pair + 2, :, :],
+                    out=h_grouped_words[:, a0 : a0 + n_tiles, :, :],
                     in_=hT_ps[:].rearrange("q a u b -> q a b u"),
                 )
-            h_codes = work.tile([P, CHUNK], U32, name="h_codes", align_bytes=64)
-            h_scales = work.tile([P, CHUNK], U8, name="h_scales", align_bytes=64)
+            h_codes = work.tile([P, n_rows], U32, name="h_codes", align_bytes=64)
+            h_scales = work.tile([P, n_rows], U8, name="h_scales", align_bytes=64)
             nc.vector.quantize_mx(out=h_codes[:].bitcast(FP8X4), scales=h_scales[:], in_=h_grouped[:])
 
-            e1_grouped = work.tile([P, CHUNK, PACK], BF16, name="e1_grouped", align_bytes=64)
-            for a in range(ROW_TILES):
+            e1_grouped = work.tile([P, n_rows, PACK], BF16, name="e1_grouped", align_bytes=64)
+            for a in range(row_tiles):
                 cols = slice(a * P, (a + 1) * P)
                 e1_ps = psum.tile([P, PACK, P], F32, name="e1_ps", tag="e1_ps")
                 for t in range(PACK):
@@ -172,23 +187,23 @@ def tile_variableselectionnetwork_pa_t_kernel(
                     in1=cb1_cols.unsqueeze(1).to_broadcast([P, P, PACK]),
                     op=ALU.add,
                 )
-            e1_codes = work.tile([P, CHUNK], U32, name="e1_codes", align_bytes=64)
-            e1_scales = work.tile([P, CHUNK], U8, name="e1_scales", align_bytes=64)
+            e1_codes = work.tile([P, n_rows], U32, name="e1_codes", align_bytes=64)
+            e1_scales = work.tile([P, n_rows], U8, name="e1_scales", align_bytes=64)
             nc.vector.quantize_mx(
                 out=e1_codes[:].bitcast(FP8X4),
                 scales=e1_scales[:],
                 in_=e1_grouped[:].rearrange("p b t -> p (b t)"),
             )
 
-            gT = gate.tile([P, FEAT_TILES, CHUNK], F32, name="gT")
+            gT = gate.tile([P, FEAT_TILES, n_rows], F32, name="gT")
             for j2 in range(0, FEAT_TILES, 2):
-                tanh_sb = gate.tile([P, 2, CHUNK], F32, name="tanh_sb")
-                half_lin_sb = gate.tile([P, 2, CHUNK], F32, name="half_lin_sb")
+                tanh_sb = gate.tile([P, 2, n_rows], F32, name="tanh_sb")
+                half_lin_sb = gate.tile([P, 2, n_rows], F32, name="half_lin_sb")
                 for i in range(2):
                     j = j2 + i
                     feats = slice(j * P, (j + 1) * P)
-                    u4_ps = psum.tile([P, CHUNK], F32, name="u4_ps", tag="u_ps")
-                    u5_ps = psum.tile([P, CHUNK], F32, name="u5_ps", tag="u_ps")
+                    u4_ps = psum.tile([P, n_rows], F32, name="u4_ps", tag="u_ps")
+                    u5_ps = psum.tile([P, n_rows], F32, name="u5_ps", tag="u_ps")
                     for u_ps, codes, scales in ((u4_ps, w4_codes, w4_scales), (u5_ps, w5_codes, w5_scales)):
                         nc.tensor.matmul_mx(
                             out=u_ps[:],
@@ -213,10 +228,10 @@ def tile_variableselectionnetwork_pa_t_kernel(
                     out=gT[:, j2 : j2 + 2, :], in0=tanh_sb[:], scalar=1.0, in1=half_lin_sb[:], op0=ALU.add, op1=ALU.mult
                 )
 
-            r_sb = tail.tile([P, ROW_TILES, WIDTH], F32, name="r_sb")
-            r_sum = tail.tile([P, ROW_TILES], F32, name="r_sum")
-            for a in range(ROW_TILES):
-                r_ps = psum.tile([P, WIDTH], F32, name="r_ps", tag="r_ps", bufs=3)
+            r_sb = tail.tile([P, row_tiles, WIDTH], F32, name="r_sb")
+            r_sum = tail.tile([P, row_tiles], F32, name="r_sum")
+            for a in range(row_tiles):
+                r_ps = psum.tile([P, WIDTH], F32, name="r_ps", tag="r_ps")
                 for j in range(FEAT_TILES):
                     feats = slice(j * P, (j + 1) * P)
                     nc.tensor.matmul(
@@ -234,30 +249,31 @@ def tile_variableselectionnetwork_pa_t_kernel(
                     out=r_sb[:, a, :], in_=r_ps[:], func=ACT.Identity, accum_out=r_sum[:, a : a + 1]
                 )
 
-            neg_mean = tail.tile([P, ROW_TILES], F32, name="neg_mean")
-            nc.gpsimd.tensor_scalar(
-                out=neg_mean[:], in0=r_sum[:], scalar1=-1.0 / WIDTH, scalar2=0.0, op0=ALU.mult, op1=ALU.add
-            )
-            squares = tail.tile([P, ROW_TILES, WIDTH], BF16, name="squares")
-            dev_sq_sum = tail.tile([P, ROW_TILES], F32, name="dev_sq_sum")
-            for a in range(ROW_TILES):
+            neg_mean = tail.tile([P, row_tiles], F32, name="neg_mean")
+            squares = tail.tile([P, row_tiles, WIDTH], BF16, name="squares")
+            dev_sq_sum = tail.tile([P, row_tiles], F32, name="dev_sq_sum")
+            var_eps = tail.tile([P, row_tiles], F32, name="var_eps")
+            rstd = tail.tile([P, row_tiles], F32, name="rstd")
+            for a in range(row_tiles):
+                one = slice(a, a + 1)
+                nc.gpsimd.tensor_scalar(
+                    out=neg_mean[:, one], in0=r_sum[:, one], scalar1=-1.0 / WIDTH, scalar2=0.0, op0=ALU.mult, op1=ALU.add
+                )
                 nc.scalar.activation(
                     out=squares[:, a, :],
                     in_=r_sb[:, a, :],
                     func=ACT.Square,
-                    bias=neg_mean[:, a : a + 1],
+                    bias=neg_mean[:, one],
                     scale=1.0,
-                    accum_out=dev_sq_sum[:, a : a + 1],
+                    accum_out=dev_sq_sum[:, one],
                 )
-            var_eps = tail.tile([P, ROW_TILES], F32, name="var_eps")
-            nc.gpsimd.tensor_scalar(
-                out=var_eps[:], in0=dev_sq_sum[:], scalar1=1.0 / WIDTH, scalar2=EPS, op0=ALU.mult, op1=ALU.add
-            )
-            rstd = tail.tile([P, ROW_TILES], F32, name="rstd")
-            nc.gpsimd.tensor_tensor(out=rstd[:], in0=var_eps[:], in1=neg_half[:], op=ALU.pow)
+                nc.gpsimd.tensor_scalar(
+                    out=var_eps[:, one], in0=dev_sq_sum[:, one], scalar1=1.0 / WIDTH, scalar2=EPS, op0=ALU.mult, op1=ALU.add
+                )
+                nc.gpsimd.tensor_tensor(out=rstd[:, one], in0=var_eps[:, one], in1=neg_half[:, one], op=ALU.pow)
 
-            c_sb = tail.tile([P, ROW_TILES, WIDTH], F32, name="c_sb", bufs=4)
-            for a in range(ROW_TILES):
+            c_sb = tail.tile([P, row_tiles, WIDTH], F32, name="c_sb", bufs=4)
+            for a in range(row_tiles):
                 nc.vector.scalar_tensor_tensor(
                     out=c_sb[:, a, :],
                     in0=r_sb[:, a, :],
@@ -266,7 +282,7 @@ def tile_variableselectionnetwork_pa_t_kernel(
                     op0=ALU.add,
                     op1=ALU.mult,
                 )
-            for a in range(ROW_TILES):
+            for a in range(row_tiles):
                 nc.vector.scalar_tensor_tensor(
                     out=c_sb[:, a, :],
                     in0=c_sb[:, a, :],
@@ -276,30 +292,53 @@ def tile_variableselectionnetwork_pa_t_kernel(
                     op1=ALU.add,
                 )
 
-            c_max = tail.tile([P, ROW_TILES, D_FEAT], BF16, name="c_max")
-            over_the_variables(c_sb, ALU.max, BF16, "c_max", c_max[:])
+            c_max = max_over_variables(c_sb, row_tiles)
             nc.vector.tensor_tensor(
                 out=by_variable(c_sb[:]), in0=by_variable(c_sb[:]), in1=over_variables(c_max[:]), op=ALU.subtract
             )
             nc.scalar.activation(out=c_sb[:], in_=c_sb[:], func=ACT.Exp)
-            over_the_variables(c_sb, ALU.add, F32, "e_sum", e_sum)
-            return c_sb
 
-        for first in range(0, N_CHUNKS, 2):
-            e_sum_inv = tail.tile([P, 2, ROW_TILES, D_FEAT], F32, name="e_sum_inv")
-            exponentials = [chunk_to_exponentials(first + i, e_sum_inv[:, i, :, :]) for i in range(2)]
-            nc.scalar.activation(out=e_sum_inv[:], in_=e_sum_inv[:], func=ACT.Ln)
+            e_sumT_ps = psum.tile([P, row_tiles, P], F32, name="e_sumT_ps", tag="e_sum_ps", bufs=1)
+            for a in range(row_tiles):
+                for j in range(FEAT_TILES):
+                    nc.tensor.matmul(
+                        out=e_sumT_ps[:, a, :],
+                        lhsT=c_sb[:, a, j * P : (j + 1) * P],
+                        rhs=ident_f32[:],
+                        start=(j == 0),
+                        stop=(j == FEAT_TILES - 1),
+                        is_transpose=True,
+                    )
+            e_sumT = tail.tile([P, row_tiles, P], F32, name="e_sumT", bufs=4)
+            nc.scalar.copy(out=e_sumT[:], in_=e_sumT_ps[:])
+            return c_sb, e_sumT
+
+        for first in range(0, len(sizes), 2):
+            pair = (first, first + 1)
+            exponentials = [chunk_to_exponentials(c) for c in pair]
+            e_sum_inv = tail.tile([P, sizes[first] + sizes[first + 1], D_FEAT], F32, name="e_sum_inv")
+            inv_of = (e_sum_inv[:, 0 : sizes[first], :], e_sum_inv[:, sizes[first] :, :])
+            for i, c in enumerate(pair):
+                e_sumT = exponentials[i][1]
+                e_sum_ps = psum.tile([P, sizes[c], P], F32, name="e_sum_ps", tag="e_sum_ps", bufs=1)
+                for a in range(sizes[c]):
+                    for moving, first_of_group in ((ident_f32, True), (swap_f32, False)):
+                        nc.tensor.matmul(
+                            out=e_sum_ps[:, a, :],
+                            lhsT=e_sumT[:, a, :],
+                            rhs=moving[:],
+                            start=first_of_group,
+                            stop=not first_of_group,
+                            is_transpose=True,
+                        )
+                nc.scalar.activation(out=inv_of[i], in_=e_sum_ps[:, :, 0:D_FEAT], func=ACT.Ln)
             nc.scalar.activation(out=e_sum_inv[:], in_=e_sum_inv[:], func=ACT.Exp, scale=-1.0)
-            for i in range(2):
-                c = first + i
-                out_sb = tail.tile([P, ROW_TILES, WIDTH], F32, name="out_sb")
+            for i, c in enumerate(pair):
+                out_sb = tail.tile([P, sizes[c], WIDTH], F32, name="out_sb")
                 nc.vector.tensor_tensor(
                     out=by_variable(out_sb[:]),
-                    in0=by_variable(exponentials[i][:]),
-                    in1=over_variables(e_sum_inv[:, i, :, :]),
+                    in0=by_variable(exponentials[i][0][:]),
+                    in1=over_variables(inv_of[i]),
                     op=ALU.mult,
                 )
-                nc.sync.dma_start(
-                    out=out[c * CHUNK : (c + 1) * CHUNK, :, :].rearrange("(p a) n d -> p a (n d)", a=ROW_TILES),
-                    in_=out_sb[:],
-                )
+                nc.sync.dma_start(out=rows_of(out, c), in_=out_sb[:])

from contextlib import ExitStack

import concourse.mybir as mybir
from concourse.masks import make_identity

F32 = mybir.dt.float32
BF16 = mybir.dt.bfloat16
U32 = mybir.dt.uint32
U8 = mybir.dt.uint8
FP8X4 = mybir.dt.float8_e4m3fn_x4
ALU = mybir.AluOpType
ACT = mybir.ActivationFunctionType

P = 128
PACK = 4
B = 4096
WIDTH = 512
N_VAR = 8
D_FEAT = 64
FEAT_TILES = WIDTH // P
MAX_ROW_TILES = 4
EPS = 1e-5

FLOPS = 3 * 2 * B * WIDTH * WIDTH


def chunk_row_tiles():
    ramp = [1]
    while sum(ramp) < MAX_ROW_TILES:
        ramp.append(sum(ramp))
    n_full = (B // P - sum(ramp)) // MAX_ROW_TILES
    return [MAX_ROW_TILES] * n_full + list(reversed(ramp))


def tile_variableselectionnetwork_pa_t_kernel(
    tc, h, x, cW1, cb1, cW4, cb4, cW5, cb5, clng, clnb, out
):
    nc = tc.nc
    sizes = chunk_row_tiles()
    first_rows = [P * sum(sizes[:c]) for c in range(len(sizes))]
    with ExitStack() as ctx:
        consts = ctx.enter_context(tc.tile_pool(name="consts", bufs=1))
        setup = ctx.enter_context(tc.tile_pool(name="setup", bufs=1))
        io = ctx.enter_context(tc.tile_pool(name="io", bufs=3))
        work = ctx.enter_context(tc.tile_pool(name="work", bufs=2))
        gate = ctx.enter_context(tc.tile_pool(name="gate", bufs=2))
        tail = ctx.enter_context(tc.tile_pool(name="tail", bufs=2))
        psum = ctx.enter_context(tc.psum_pool(name="psum", bufs=2))

        def rows_of(dram, c):
            rows = slice(first_rows[c], first_rows[c] + P * sizes[c])
            if dram.ndim == 3:
                return dram[rows, :, :].rearrange("(p a) n d -> p a (n d)", a=sizes[c])
            return dram[rows, :].rearrange("(p a) k -> p a k", a=sizes[c])

        def load_chunk(c):
            h_sb = io.tile([P, sizes[c], WIDTH], BF16, name="h_sb", tag="h_sb")
            nc.sync.dma_start(out=h_sb[:], in_=rows_of(h, c))
            x_sb = io.tile([P, sizes[c], WIDTH], BF16, name="x_sb", tag="x_sb")
            nc.sync.dma_start(out=x_sb[:], in_=rows_of(x, c))
            return h_sb, x_sb

        loaded = {0: load_chunk(0)}
        w1_raw = setup.tile([P, PACK, WIDTH], BF16, name="w1_raw")
        nc.sync.dma_start(
            out=w1_raw[:].rearrange("q (u e) c -> q u (e c)", u=2),
            in_=cW1.rearrange("(u q e) c -> q u (e c)", u=2, e=2),
        )
        bias_rows = setup.tile([P, P], BF16, name="bias_rows")
        nc.vector.memset(bias_rows[:], 0.0)
        for i, vec in enumerate((cb1, cb4, cb5)):
            nc.sync.dma_start(
                out=bias_rows[FEAT_TILES * i : FEAT_TILES * (i + 1), :],
                in_=vec.rearrange("(t p) -> t p", p=P),
            )
        w4_raw = setup.tile([P, PACK, WIDTH], BF16, name="w4_raw")
        nc.sync.dma_start(out=w4_raw[:], in_=cW4.rearrange("(t p) c -> p t c", p=P))
        w5_raw = setup.tile([P, PACK, WIDTH], BF16, name="w5_raw")
        nc.sync.dma_start(out=w5_raw[:], in_=cW5.rearrange("(t p) c -> p t c", p=P))
        clng_bc = consts.tile([P, WIDTH], BF16, name="clng_bc")
        nc.gpsimd.dma_start(out=clng_bc[:], in_=clng.partition_broadcast(P))
        clnb_bc = consts.tile([P, WIDTH], BF16, name="clnb_bc")
        nc.gpsimd.dma_start(out=clnb_bc[:], in_=clnb.partition_broadcast(P))

        ident_f32 = consts.tile([P, P], F32, name="ident_f32")
        make_identity(nc, ident_f32[:])
        ident_bf16 = consts.tile([P, P], BF16, name="ident_bf16")
        make_identity(nc, ident_bf16[:])
        swap_f32 = consts.tile([P, P], F32, name="swap_f32")
        nc.vector.tensor_copy(out=swap_f32[:, 0:D_FEAT], in_=ident_f32[:, D_FEAT:P])
        nc.vector.tensor_copy(out=swap_f32[:, D_FEAT:P], in_=ident_f32[:, 0:D_FEAT])
        neg_half = consts.tile([P, MAX_ROW_TILES], F32, name="neg_half")
        nc.vector.memset(neg_half[:], -0.5)

        def quantise_weight(raw, copy, name):
            grouped = setup.tile([P, WIDTH, PACK], BF16, name=name + "_grouped", align_bytes=64)
            copy(
                out=grouped[:].rearrange("p (c i) t -> p c t i", i=4),
                in_=raw[:].rearrange("p t (c i) -> p c t i", i=4),
            )
            codes = consts.tile([P, WIDTH], U32, name=name + "_codes", align_bytes=64)
            scales = consts.tile([P, WIDTH], U8, name=name + "_scales", align_bytes=64)
            nc.vector.quantize_mx(
                out=codes[:].bitcast(FP8X4),
                scales=scales[:],
                in_=grouped[:].rearrange("p c t -> p (c t)"),
            )
            return codes, scales

        w1_codes, w1_scales = quantise_weight(w1_raw, nc.vector.tensor_copy, "w1")
        w4_codes, w4_scales = quantise_weight(w4_raw, nc.scalar.copy, "w4")
        w5_codes, w5_scales = quantise_weight(w5_raw, nc.scalar.copy, "w5")

        bias_ps = psum.tile([P, P], BF16, name="bias_ps", tag="hT_ps", bufs=1)
        nc.tensor.transpose(bias_ps[:], bias_rows[:], ident_bf16[:])
        bias_cols = consts.tile([P, 3 * FEAT_TILES], F32, name="bias_cols")
        nc.vector.tensor_copy(out=bias_cols[:], in_=bias_ps[:, 0 : 3 * FEAT_TILES])
        cb1_cols = bias_cols[:, 0:FEAT_TILES]
        half_cb45_cols = consts.tile([P, 2 * FEAT_TILES], F32, name="half_cb45_cols")
        nc.vector.tensor_scalar_mul(
            out=half_cb45_cols[:], in0=bias_cols[:, FEAT_TILES : 3 * FEAT_TILES], scalar1=0.5
        )
        half_cb4_cols = half_cb45_cols[:, 0:FEAT_TILES]
        half_cb5_cols = half_cb45_cols[:, FEAT_TILES : 2 * FEAT_TILES]

        def max_over_variables(src, row_tiles):
            width = WIDTH
            while width > D_FEAT:
                width //= 2
                dst = tail.tile([P, row_tiles, width], BF16, name="c_max_%d" % width)
                nc.vector.tensor_tensor(
                    out=dst[:], in0=src[:, :, 0:width], in1=src[:, :, width : 2 * width], op=ALU.max
                )
                src = dst
            return src

        def over_variables(per_feature):
            return per_feature.unsqueeze(2).to_broadcast([P, per_feature.shape[1], N_VAR, D_FEAT])

        def by_variable(tile_ap):
            return tile_ap.rearrange("p a (n d) -> p a n d", n=N_VAR)

        def chunk_to_exponentials(c):
            row_tiles = sizes[c]
            n_rows = P * row_tiles
            if c + 1 < len(sizes):
                loaded[c + 1] = load_chunk(c + 1)
            h_sb, x_sb = loaded[c]

            h_grouped = work.tile([P, n_rows * PACK], BF16, name="h_grouped", align_bytes=64)
            h_grouped_words = h_grouped[:].bitcast(F32).rearrange("q (a b u) -> q a b u", a=row_tiles, u=2)
            for a0 in range(0, row_tiles, 2):
                n_tiles = min(2, row_tiles - a0)
                hT_ps = psum.tile([P, n_tiles, 2, P], F32, name="hT_ps", tag="hT_ps", bufs=1)
                for a in range(n_tiles):
                    h_words = h_sb[:, a0 + a, :].bitcast(F32)
                    for u in range(2):
                        nc.tensor.transpose(
                            hT_ps[:, a, u, :], h_words[:, u * P : (u + 1) * P], ident_f32[:]
                        )
                nc.scalar.copy(
                    out=h_grouped_words[:, a0 : a0 + n_tiles, :, :],
                    in_=hT_ps[:].rearrange("q a u b -> q a b u"),
                )
            h_codes = work.tile([P, n_rows], U32, name="h_codes", align_bytes=64)
            h_scales = work.tile([P, n_rows], U8, name="h_scales", align_bytes=64)
            nc.vector.quantize_mx(out=h_codes[:].bitcast(FP8X4), scales=h_scales[:], in_=h_grouped[:])

            e1_grouped = work.tile([P, n_rows, PACK], BF16, name="e1_grouped", align_bytes=64)
            for a in range(row_tiles):
                cols = slice(a * P, (a + 1) * P)
                e1_ps = psum.tile([P, PACK, P], F32, name="e1_ps", tag="e1_ps")
                for t in range(PACK):
                    feats = slice(t * P, (t + 1) * P)
                    nc.tensor.matmul_mx(
                        out=e1_ps[:, t, :],
                        lhsT=w1_codes[:, feats].bitcast(FP8X4),
                        lhsT_scale=w1_scales[:, feats],
                        rhs=h_codes[:, cols].bitcast(FP8X4),
                        rhs_scale=h_scales[:, cols],
                        start=True,
                        stop=True,
                    )
                nc.vector.tensor_tensor(
                    out=e1_grouped[:, cols, :],
                    in0=e1_ps[:].rearrange("p t b -> p b t"),
                    in1=cb1_cols.unsqueeze(1).to_broadcast([P, P, PACK]),
                    op=ALU.add,
                )
            e1_codes = work.tile([P, n_rows], U32, name="e1_codes", align_bytes=64)
            e1_scales = work.tile([P, n_rows], U8, name="e1_scales", align_bytes=64)
            nc.vector.quantize_mx(
                out=e1_codes[:].bitcast(FP8X4),
                scales=e1_scales[:],
                in_=e1_grouped[:].rearrange("p b t -> p (b t)"),
            )

            gT = gate.tile([P, FEAT_TILES, n_rows], F32, name="gT")
            for j2 in range(0, FEAT_TILES, 2):
                tanh_sb = gate.tile([P, 2, n_rows], F32, name="tanh_sb")
                half_lin_sb = gate.tile([P, 2, n_rows], F32, name="half_lin_sb")
                for i in range(2):
                    j = j2 + i
                    feats = slice(j * P, (j + 1) * P)
                    u4_ps = psum.tile([P, n_rows], F32, name="u4_ps", tag="u_ps")
                    u5_ps = psum.tile([P, n_rows], F32, name="u5_ps", tag="u_ps")
                    for u_ps, codes, scales in ((u4_ps, w4_codes, w4_scales), (u5_ps, w5_codes, w5_scales)):
                        nc.tensor.matmul_mx(
                            out=u_ps[:],
                            lhsT=codes[:, feats].bitcast(FP8X4),
                            lhsT_scale=scales[:, feats],
                            rhs=e1_codes[:].bitcast(FP8X4),
                            rhs_scale=e1_scales[:],
                            start=True,
                            stop=True,
                        )
                    nc.scalar.activation(
                        out=tanh_sb[:, i, :], in_=u4_ps[:], func=ACT.Tanh, bias=half_cb4_cols[:, j : j + 1], scale=0.5
                    )
                    nc.scalar.activation(
                        out=half_lin_sb[:, i, :],
                        in_=u5_ps[:],
                        func=ACT.Identity,
                        bias=half_cb5_cols[:, j : j + 1],
                        scale=0.5,
                    )
                nc.vector.scalar_tensor_tensor(
                    out=gT[:, j2 : j2 + 2, :], in0=tanh_sb[:], scalar=1.0, in1=half_lin_sb[:], op0=ALU.add, op1=ALU.mult
                )

            r_sb = tail.tile([P, row_tiles, WIDTH], F32, name="r_sb")
            r_sum = tail.tile([P, row_tiles], F32, name="r_sum")
            for a in range(row_tiles):
                r_ps = psum.tile([P, WIDTH], F32, name="r_ps", tag="r_ps")
                for j in range(FEAT_TILES):
                    feats = slice(j * P, (j + 1) * P)
                    nc.tensor.matmul(
                        out=r_ps[:, feats], lhsT=ident_bf16[:], rhs=x_sb[:, a, feats], start=True, stop=False
                    )
                    nc.tensor.matmul(
                        out=r_ps[:, feats],
                        lhsT=gT[:, j, a * P : (a + 1) * P],
                        rhs=ident_f32[:],
                        start=False,
                        stop=True,
                        is_transpose=True,
                    )
                nc.scalar.activation(
                    out=r_sb[:, a, :], in_=r_ps[:], func=ACT.Identity, accum_out=r_sum[:, a : a + 1]
                )

            neg_mean = tail.tile([P, row_tiles], F32, name="neg_mean")
            squares = tail.tile([P, row_tiles, WIDTH], BF16, name="squares")
            dev_sq_sum = tail.tile([P, row_tiles], F32, name="dev_sq_sum")
            var_eps = tail.tile([P, row_tiles], F32, name="var_eps")
            rstd = tail.tile([P, row_tiles], F32, name="rstd")
            for a in range(row_tiles):
                one = slice(a, a + 1)
                nc.gpsimd.tensor_scalar(
                    out=neg_mean[:, one], in0=r_sum[:, one], scalar1=-1.0 / WIDTH, scalar2=0.0, op0=ALU.mult, op1=ALU.add
                )
                nc.scalar.activation(
                    out=squares[:, a, :],
                    in_=r_sb[:, a, :],
                    func=ACT.Square,
                    bias=neg_mean[:, one],
                    scale=1.0,
                    accum_out=dev_sq_sum[:, one],
                )
                nc.gpsimd.tensor_scalar(
                    out=var_eps[:, one], in0=dev_sq_sum[:, one], scalar1=1.0 / WIDTH, scalar2=EPS, op0=ALU.mult, op1=ALU.add
                )
                nc.gpsimd.tensor_tensor(out=rstd[:, one], in0=var_eps[:, one], in1=neg_half[:, one], op=ALU.pow)

            c_sb = tail.tile([P, row_tiles, WIDTH], F32, name="c_sb", bufs=4)
            for a in range(row_tiles):
                nc.vector.scalar_tensor_tensor(
                    out=c_sb[:, a, :],
                    in0=r_sb[:, a, :],
                    scalar=neg_mean[:, a : a + 1],
                    in1=clng_bc[:],
                    op0=ALU.add,
                    op1=ALU.mult,
                )
            for a in range(row_tiles):
                nc.vector.scalar_tensor_tensor(
                    out=c_sb[:, a, :],
                    in0=c_sb[:, a, :],
                    scalar=rstd[:, a : a + 1],
                    in1=clnb_bc[:],
                    op0=ALU.mult,
                    op1=ALU.add,
                )

            c_max = max_over_variables(c_sb, row_tiles)
            nc.vector.tensor_tensor(
                out=by_variable(c_sb[:]), in0=by_variable(c_sb[:]), in1=over_variables(c_max[:]), op=ALU.subtract
            )
            nc.scalar.activation(out=c_sb[:], in_=c_sb[:], func=ACT.Exp)

            e_sumT_ps = psum.tile([P, row_tiles, P], F32, name="e_sumT_ps", tag="e_sum_ps", bufs=1)
            for a in range(row_tiles):
                for j in range(FEAT_TILES):
                    nc.tensor.matmul(
                        out=e_sumT_ps[:, a, :],
                        lhsT=c_sb[:, a, j * P : (j + 1) * P],
                        rhs=ident_f32[:],
                        start=(j == 0),
                        stop=(j == FEAT_TILES - 1),
                        is_transpose=True,
                    )
            e_sumT = tail.tile([P, row_tiles, P], F32, name="e_sumT", bufs=4)
            nc.scalar.copy(out=e_sumT[:], in_=e_sumT_ps[:])
            return c_sb, e_sumT

        for first in range(0, len(sizes), 2):
            pair = (first, first + 1)
            exponentials = [chunk_to_exponentials(c) for c in pair]
            e_sum_inv = tail.tile([P, sizes[first] + sizes[first + 1], D_FEAT], F32, name="e_sum_inv")
            inv_of = (e_sum_inv[:, 0 : sizes[first], :], e_sum_inv[:, sizes[first] :, :])
            for i, c in enumerate(pair):
                e_sumT = exponentials[i][1]
                e_sum_ps = psum.tile([P, sizes[c], P], F32, name="e_sum_ps", tag="e_sum_ps", bufs=1)
                for a in range(sizes[c]):
                    for moving, first_of_group in ((ident_f32, True), (swap_f32, False)):
                        nc.tensor.matmul(
                            out=e_sum_ps[:, a, :],
                            lhsT=e_sumT[:, a, :],
                            rhs=moving[:],
                            start=first_of_group,
                            stop=not first_of_group,
                            is_transpose=True,
                        )
                nc.scalar.activation(out=inv_of[i], in_=e_sum_ps[:, :, 0:D_FEAT], func=ACT.Ln)
            nc.scalar.activation(out=e_sum_inv[:], in_=e_sum_inv[:], func=ACT.Exp, scale=-1.0)
            for i, c in enumerate(pair):
                out_sb = tail.tile([P, sizes[c], WIDTH], F32, name="out_sb")
                nc.vector.tensor_tensor(
                    out=by_variable(out_sb[:]),
                    in0=by_variable(exponentials[i][0][:]),
                    in1=over_variables(inv_of[i]),
                    op=ALU.mult,
                )
                nc.sync.dma_start(out=rows_of(out, c), in_=out_sb[:])
